import numpy as np
import ml_dtypes


def mxq(x, axis, fmt="e4m3"):
    dtype, down = {"e4m3": (ml_dtypes.float8_e4m3fn, 7), "e5m2": (ml_dtypes.float8_e5m2, 14)}[fmt]
    v = np.moveaxis(np.asarray(x, np.float32).astype(ml_dtypes.bfloat16).astype(np.float64), axis, -1)
    blocks = v.reshape(v.shape[:-1] + (-1, 32))
    amax = np.abs(blocks).max(-1, keepdims=True)
    byte = np.maximum(np.where(amax > 0, np.frexp(amax)[1] - 1 + 127, 0) - down, 1)
    scale = np.exp2(byte - 127.0)
    codes = (blocks / scale).astype(np.float32).astype(dtype).astype(np.float64)
    return np.moveaxis((codes * scale).reshape(v.shape), -1, axis)


WIDE = False


def mx_kscale(k):
    if not WIDE:
        return np.ones(k)
    levels = np.array([10, -10, 5, -5, 0])
    a = np.random.permutation(np.resize(levels, k // 512 * 4)).reshape(k // 512, 4)
    idx = np.arange(k)
    return np.exp2(a[idx // 512, idx % 128 // 32])


BF16 = ml_dtypes.bfloat16


def bf(x):
    return np.asarray(x, np.float32).astype(BF16)


def f64(x):
    return np.asarray(x).astype(np.float64)


B, I, O, M = 1024, 512, 256, 2


def modemul(a, c):
    return (a.transpose(2, 3, 4, 0, 1) @ c.transpose(2, 3, 4, 0, 1)).transpose(3, 4, 0, 1, 2)


def setup_inputs():
    s = mx_kscale(I)
    sx = s[None, :, None, None, None]
    sw = s[:, None, None, None, None]
    xs, ws = (B, I, M, M, M), (I, O, M, M, M)
    return {"x_real": bf(np.random.standard_normal(xs) * sx),
            "x_imag": bf(np.random.standard_normal(xs) * sx),
            "w_real": bf(np.random.standard_normal(ws) / np.sqrt(I) / sw),
            "w_imag": bf(np.random.standard_normal(ws) / np.sqrt(I) / sw)}


def reference(x_real, x_imag, w_real, w_imag):
    xr, xi = mxq(f64(x_real), 1, "e4m3"), mxq(f64(x_imag), 1, "e4m3")
    wr, wi = mxq(f64(w_real), 0, "e4m3"), mxq(f64(w_imag), 0, "e4m3")
    re = modemul(xr, wr) - modemul(xi, wi)
    im = modemul(xr, wi) + modemul(xi, wr)
    return np.stack([re, im])

@@ -1,0 +1,182 @@
+from contextlib import ExitStack
+
+import concourse.bass as bass
+import concourse.mybir as mybir
+import concourse.tile as tile
+from concourse.masks import make_identity
+
+F32 = mybir.dt.float32
+BF16 = mybir.dt.bfloat16
+U32 = mybir.dt.uint32
+U8 = mybir.dt.uint8
+FP8X4 = mybir.dt.float8_e4m3fn_x4
+
+P = 128
+B, I, O, NM = 1024, 512, 256, 8
+NBT = B // P
+FLOPS = 2 * 4 * NM * B * I * O
+
+XBUFS = 4
+
+
+def tile_mymodel_t_kernel(tc, x_real, x_imag, w_real, w_imag, out):
+    nc = tc.nc
+    xs_dram = [
+        x_real.rearrange("b i x y z -> b (i x y z)"),
+        x_imag.rearrange("b i x y z -> b (i x y z)"),
+    ]
+    w_dram = {
+        "r": w_real.rearrange("(t p) o x y z -> p t (o x y z)", p=P),
+        "i": w_imag.rearrange("(t p) o x y z -> p t (o x y z)", p=P),
+    }
+    out_dram = out.rearrange("c b o x y z -> b c (o x y z)")
+
+    with ExitStack() as ctx:
+        const = ctx.enter_context(tc.tile_pool(name="const", bufs=1))
+        xpool = ctx.enter_context(tc.tile_pool(name="xpool", bufs=XBUFS))
+        wpool = ctx.enter_context(tc.tile_pool(name="wpool", bufs=1))
+        gpool = ctx.enter_context(tc.tile_pool(name="gpool", bufs=2))
+        cpool = ctx.enter_context(tc.tile_pool(name="cpool", bufs=6))
+        opool = ctx.enter_context(tc.tile_pool(name="opool", bufs=4))
+        ps_t = ctx.enter_context(tc.psum_pool(name="ps_t", bufs=4))
+        ps_o = ctx.enter_context(tc.psum_pool(name="ps_o", bufs=4))
+        ctx.enter_context(tc.manual_schedule())
+
+        ident = const.tile([P, P], F32, name="ident")
+        make_identity(nc, ident[:])
+
+        x_tiles = {}
+
+        def load_x(bt):
+            pair = []
+            for s in range(2):
+                xt = xpool.tile([P, I * NM], BF16, name="x%d" % s, tag="x%d" % s)
+                nc.sync.dma_start(out=xt[:], in_=xs_dram[s][bt * P : (bt + 1) * P, :])
+                pair.append(xt)
+            x_tiles[bt] = pair
+
+        w_raw = {}
+
+        def load_w(v, oh):
+            wt = wpool.tile([P, 4, P * NM], BF16, name="wraw_%s%d" % (v, oh))
+            nc.sync.dma_start(out=wt[:], in_=w_dram[v][:, :, oh * P * NM : (oh + 1) * P * NM])
+            w_raw[(v, oh)] = wt
+
+        w_codes = {}
+        w_scales = {}
+        for v in ("r", "i", "n"):
+            for oh in range(2):
+                w_codes[(v, oh)] = wpool.tile([P, NM * P], U32, name="wc_%s%d" % (v, oh), align_bytes=64)
+                w_scales[(v, oh)] = wpool.tile([P, NM * P], U8, name="ws_%s%d" % (v, oh), align_bytes=64)
+
+        def regroup_w(eng, dst, src, m0, m1):
+            o_ap = dst[:, m0 * 512 : m1 * 512].rearrange("p (m o t) -> p m o t", o=P, t=4)
+            i_ap = src[:].rearrange("p t (o m) -> p m o t", m=NM)[:, m0:m1]
+            if eng == "v":
+                nc.vector.tensor_copy(out=o_ap, in_=i_ap)
+            else:
+                nc.scalar.copy(out=o_ap, in_=i_ap)
+
+        def quant_w(v, oh, grouped):
+            nc.vector.quantize_mx(
+                out=w_codes[(v, oh)][:].bitcast(FP8X4),
+                scales=w_scales[(v, oh)][:],
+                in_=grouped[:],
+            )
+
+        def prep_w(oh):
+            gi = wpool.tile([P, NM * P * 4], BF16, name="g_i", tag="g_i", align_bytes=64)
+            gn = wpool.tile([P, NM * P * 4], BF16, name="g_n", tag="g_n", align_bytes=64)
+            gr = wpool.tile([P, NM * P * 4], BF16, name="g_r", tag="g_r", align_bytes=64)
+            regroup_w("v", gi, w_raw[("i", oh)], 0, 4)
+            regroup_w("s", gi, w_raw[("i", oh)], 4, 8)
+            regroup_w("v", gr, w_raw[("r", oh)], 0, 2)
+            regroup_w("s", gr, w_raw[("r", oh)], 2, 8)
+            quant_w("i", oh, gi)
+            nc.vector.tensor_scalar_mul(out=gn[:], in0=gi[:], scalar1=-1.0)
+            quant_w("n", oh, gn)
+            quant_w("r", oh, gr)
+
+        x_codes = {}
+
+        def tau(u):
+            bt, h = u // 2, u % 2
+            grouped = gpool.tile([P, 4096], BF16, name="grouped", align_bytes=64)
+            banks = []
+            for s in range(2):
+                xw = x_tiles[bt][s][:].bitcast(F32).rearrange("p (i q) -> p i q", q=4)
+                for mpl in range(2):
+                    tb = ps_t.tile([P, 512], F32, name="tb")
+                    for t in range(4):
+                        nc.tensor.transpose(
+                            tb[:, t * P : (t + 1) * P],
+                            xw[:, t * P : (t + 1) * P, 2 * h + mpl],
+                            ident[:],
+                        )
+                    banks.append(tb)
+            for k in range(4):
+                o_ap = grouped[:, k * 1024 : (k + 1) * 1024].rearrange("p (e b t) -> p e b t", e=2, t=4)
+                i_ap = banks[k][:].bitcast(BF16).rearrange("p (t b e) -> p e b t", t=4, e=2)
+                if k % 2 == 0:
+                    nc.scalar.copy(out=o_ap, in_=i_ap)
+                else:
+                    nc.vector.tensor_copy(out=o_ap, in_=i_ap)
+            xc = cpool.tile([P, 1024], U32, name="xc", align_bytes=64)
+            xsc = cpool.tile([P, 1024], U8, name="xsc", align_bytes=64)
+            nc.vector.quantize_mx(out=xc[:].bitcast(FP8X4), scales=xsc[:], in_=grouped[:])
+            x_codes[u] = (xc, xsc)
+
+        def mu(j):
+            bt, oh = j // 2, j % 2
+            ot = opool.tile([P, 2, P, NM], F32, name="ot")
+            for c in (1, 0):
+                for h in range(2):
+                    xc, xsc = x_codes[2 * bt + h]
+                    ob = ps_o.tile([P, 512], F32, name="ob")
+                    for ml in range(4):
+                        m = 4 * h + ml
+                        pairs = ((0, "r"), (1, "n")) if c == 0 else ((0, "i"), (1, "r"))
+                        for n, (s, v) in enumerate(pairs):
+                            sl = slice((4 * s + ml) * P, (4 * s + ml + 1) * P)
+                            wl = slice(m * P, (m + 1) * P)
+                            nc.tensor.matmul_mx(
+                                out=ob[:, ml * P : (ml + 1) * P],
+                                lhsT=xc[:, sl].bitcast(FP8X4),
+                                lhsT_scale=xsc[:, sl],
+                                rhs=w_codes[(v, oh)][:, wl].bitcast(FP8X4),
+                                rhs_scale=w_scales[(v, oh)][:, wl],
+                                start=(n == 0),
+                                stop=(n == 1),
+                            )
+                    o_ap = ot[:, c, :, 4 * h : 4 * h + 4]
+                    i_ap = ob[:].rearrange("p (m o) -> p o m", m=4)
+                    if c == 0 and j % 2 == 0:
+                        nc.vector.tensor_copy(out=o_ap, in_=i_ap)
+                    else:
+                        nc.scalar.copy(out=o_ap, in_=i_ap)
+            nc.sync.dma_start(
+                out=out_dram[bt * P : (bt + 1) * P, :, oh * P * NM : (oh + 1) * P * NM],
+                in_=ot[:].rearrange("p c o m -> p c (o m)"),
+            )
+
+        load_x(0)
+        load_w("i", 0)
+        load_w("r", 0)
+        load_x(1)
+        load_w("i", 1)
+        load_w("r", 1)
+        load_x(2)
+        load_x(3)
+
+        tau(0)
+        tau(1)
+        prep_w(0)
+        tau(2)
+        for j in range(2 * NBT):
+            if 1 <= j and j + 2 < 2 * NBT:
+                tau(j + 2)
+            if j == 1:
+                prep_w(1)
+            mu(j)
+            if j % 2 == 1 and j // 2 + XBUFS < NBT:
+                load_x(j // 2 + XBUFS)

@@ -1,8 +1,6 @@
 from contextlib import ExitStack
 
-import concourse.bass as bass
 import concourse.mybir as mybir
-import concourse.tile as tile
 from concourse.masks import make_identity
 
 F32 = mybir.dt.float32
@@ -10,13 +8,13 @@ BF16 = mybir.dt.bfloat16
 U32 = mybir.dt.uint32
 U8 = mybir.dt.uint8
 FP8X4 = mybir.dt.float8_e4m3fn_x4
+MULT = mybir.AluOpType.mult
+ADD = mybir.AluOpType.add
 
 P = 128
 B, I, O, NM = 1024, 512, 256, 8
 NBT = B // P
 FLOPS = 2 * 4 * NM * B * I * O
-
-XBUFS = 4
 
 
 def tile_mymodel_t_kernel(tc, x_real, x_imag, w_real, w_imag, out):
@@ -33,10 +31,10 @@ def tile_mymodel_t_kernel(tc, x_real, x_imag, w_real, w_imag, out):
 
     with ExitStack() as ctx:
         const = ctx.enter_context(tc.tile_pool(name="const", bufs=1))
-        xpool = ctx.enter_context(tc.tile_pool(name="xpool", bufs=XBUFS))
+        big = ctx.enter_context(tc.tile_pool(name="big", bufs=10))
         wpool = ctx.enter_context(tc.tile_pool(name="wpool", bufs=1))
         gpool = ctx.enter_context(tc.tile_pool(name="gpool", bufs=2))
-        cpool = ctx.enter_context(tc.tile_pool(name="cpool", bufs=6))
+        cpool = ctx.enter_context(tc.tile_pool(name="cpool", bufs=8))
         opool = ctx.enter_context(tc.tile_pool(name="opool", bufs=4))
         ps_t = ctx.enter_context(tc.psum_pool(name="ps_t", bufs=4))
         ps_o = ctx.enter_context(tc.psum_pool(name="ps_o", bufs=4))
@@ -48,17 +46,15 @@ def tile_mymodel_t_kernel(tc, x_real, x_imag, w_real, w_imag, out):
         x_tiles = {}
 
         def load_x(bt):
-            pair = []
             for s in range(2):
-                xt = xpool.tile([P, I * NM], BF16, name="x%d" % s, tag="x%d" % s)
+                xt = big.tile([P, I * NM], BF16, name="xt", tag="big")
                 nc.sync.dma_start(out=xt[:], in_=xs_dram[s][bt * P : (bt + 1) * P, :])
-                pair.append(xt)
-            x_tiles[bt] = pair
+                x_tiles[(bt, s)] = xt
 
         w_raw = {}
 
         def load_w(v, oh):
-            wt = wpool.tile([P, 4, P * NM], BF16, name="wraw_%s%d" % (v, oh))
+            wt = big.tile([P, 4, P * NM], BF16, name="wt", tag="big")
             nc.sync.dma_start(out=wt[:], in_=w_dram[v][:, :, oh * P * NM : (oh + 1) * P * NM])
             w_raw[(v, oh)] = wt
 
@@ -69,33 +65,35 @@ def tile_mymodel_t_kernel(tc, x_real, x_imag, w_real, w_imag, out):
                 w_codes[(v, oh)] = wpool.tile([P, NM * P], U32, name="wc_%s%d" % (v, oh), align_bytes=64)
                 w_scales[(v, oh)] = wpool.tile([P, NM * P], U8, name="ws_%s%d" % (v, oh), align_bytes=64)
 
-        def regroup_w(eng, dst, src, m0, m1):
-            o_ap = dst[:, m0 * 512 : m1 * 512].rearrange("p (m o t) -> p m o t", o=P, t=4)
-            i_ap = src[:].rearrange("p t (o m) -> p m o t", m=NM)[:, m0:m1]
+        w_grouped = {}
+
+        def regroup_w(eng, v, oh, h):
+            g = wpool.tile([P, 2048], BF16, name="g_%s%d" % (v, h), align_bytes=64)
+            w_grouped[(v, oh, h)] = g
+            o_ap = g[:].rearrange("p (m o t) -> p o t m", m=4, t=4)
+            i_ap = w_raw[(v, oh)][:].rearrange("p t (o m) -> p o t m", m=NM)[:, :, :, 4 * h : 4 * h + 4]
             if eng == "v":
                 nc.vector.tensor_copy(out=o_ap, in_=i_ap)
-            else:
+            elif eng == "s":
                 nc.scalar.copy(out=o_ap, in_=i_ap)
+            else:
+                nc.gpsimd.tensor_scalar(out=o_ap, in0=i_ap, scalar1=1.0, scalar2=0.0, op0=MULT, op1=ADD)
 
-        def quant_w(v, oh, grouped):
+        def quant_w(v, oh, h):
+            cols = slice(h * 512, (h + 1) * 512)
             nc.vector.quantize_mx(
-                out=w_codes[(v, oh)][:].bitcast(FP8X4),
-                scales=w_scales[(v, oh)][:],
-                in_=grouped[:],
+                out=w_codes[(v, oh)][:, cols].bitcast(FP8X4),
+                scales=w_scales[(v, oh)][:, cols],
+                in_=w_grouped[(v, oh, h)][:],
             )
 
-        def prep_w(oh):
-            gi = wpool.tile([P, NM * P * 4], BF16, name="g_i", tag="g_i", align_bytes=64)
-            gn = wpool.tile([P, NM * P * 4], BF16, name="g_n", tag="g_n", align_bytes=64)
-            gr = wpool.tile([P, NM * P * 4], BF16, name="g_r", tag="g_r", align_bytes=64)
-            regroup_w("v", gi, w_raw[("i", oh)], 0, 4)
-            regroup_w("s", gi, w_raw[("i", oh)], 4, 8)
-            regroup_w("v", gr, w_raw[("r", oh)], 0, 2)
-            regroup_w("s", gr, w_raw[("r", oh)], 2, 8)
-            quant_w("i", oh, gi)
-            nc.vector.tensor_scalar_mul(out=gn[:], in0=gi[:], scalar1=-1.0)
-            quant_w("n", oh, gn)
-            quant_w("r", oh, gr)
+        def quant_w_half(oh, h):
+            quant_w("i", oh, h)
+            gn = wpool.tile([P, 2048], BF16, name="g_n%d" % h, align_bytes=64)
+            w_grouped[("n", oh, h)] = gn
+            nc.vector.tensor_scalar_mul(out=gn[:], in0=w_grouped[("i", oh, h)][:], scalar1=-1.0)
+            quant_w("r", oh, h)
+            quant_w("n", oh, h)
 
         x_codes = {}
 
@@ -104,7 +102,7 @@ def tile_mymodel_t_kernel(tc, x_real, x_imag, w_real, w_imag, out):
             grouped = gpool.tile([P, 4096], BF16, name="grouped", align_bytes=64)
             banks = []
             for s in range(2):
-                xw = x_tiles[bt][s][:].bitcast(F32).rearrange("p (i q) -> p i q", q=4)
+                xw = x_tiles[(bt, s)][:].bitcast(F32).rearrange("p (i q) -> p i q", q=4)
                 for mpl in range(2):
                     tb = ps_t.tile([P, 512], F32, name="tb")
                     for t in range(4):
@@ -117,47 +115,54 @@ def tile_mymodel_t_kernel(tc, x_real, x_imag, w_real, w_imag, out):
             for k in range(4):
                 o_ap = grouped[:, k * 1024 : (k + 1) * 1024].rearrange("p (e b t) -> p e b t", e=2, t=4)
                 i_ap = banks[k][:].bitcast(BF16).rearrange("p (t b e) -> p e b t", t=4, e=2)
-                if k % 2 == 0:
-                    nc.scalar.copy(out=o_ap, in_=i_ap)
-                else:
+                on_vector = (k == 3) if u < 6 else (k % 2 == 1)
+                if on_vector:
                     nc.vector.tensor_copy(out=o_ap, in_=i_ap)
+                else:
+                    nc.scalar.copy(out=o_ap, in_=i_ap)
             xc = cpool.tile([P, 1024], U32, name="xc", align_bytes=64)
             xsc = cpool.tile([P, 1024], U8, name="xsc", align_bytes=64)
             nc.vector.quantize_mx(out=xc[:].bitcast(FP8X4), scales=xsc[:], in_=grouped[:])
             x_codes[u] = (xc, xsc)
 
-        def mu(j):
-            bt, oh = j // 2, j % 2
-            ot = opool.tile([P, 2, P, NM], F32, name="ot")
-            for c in (1, 0):
-                for h in range(2):
-                    xc, xsc = x_codes[2 * bt + h]
-                    ob = ps_o.tile([P, 512], F32, name="ob")
-                    for ml in range(4):
-                        m = 4 * h + ml
-                        pairs = ((0, "r"), (1, "n")) if c == 0 else ((0, "i"), (1, "r"))
-                        for n, (s, v) in enumerate(pairs):
-                            sl = slice((4 * s + ml) * P, (4 * s + ml + 1) * P)
-                            wl = slice(m * P, (m + 1) * P)
-                            nc.tensor.matmul_mx(
-                                out=ob[:, ml * P : (ml + 1) * P],
-                                lhsT=xc[:, sl].bitcast(FP8X4),
-                                lhsT_scale=xsc[:, sl],
-                                rhs=w_codes[(v, oh)][:, wl].bitcast(FP8X4),
-                                rhs_scale=w_scales[(v, oh)][:, wl],
-                                start=(n == 0),
-                                stop=(n == 1),
-                            )
-                    o_ap = ot[:, c, :, 4 * h : 4 * h + 4]
-                    i_ap = ob[:].rearrange("p (m o) -> p o m", m=4)
-                    if c == 0 and j % 2 == 0:
-                        nc.vector.tensor_copy(out=o_ap, in_=i_ap)
-                    else:
-                        nc.scalar.copy(out=o_ap, in_=i_ap)
+        def store(ot, bt, oh, c0, c1):
             nc.sync.dma_start(
-                out=out_dram[bt * P : (bt + 1) * P, :, oh * P * NM : (oh + 1) * P * NM],
-                in_=ot[:].rearrange("p c o m -> p c (o m)"),
+                out=out_dram[bt * P : (bt + 1) * P, c0:c1, oh * P * NM : (oh + 1) * P * NM],
+                in_=ot[:, c0:c1].rearrange("p c o m -> p c (o m)"),
             )
+
+        def mu(bt, oh, last):
+            ot = opool.tile([P, 2, P, NM], F32, name="ot")
+            order = ((1, 0), (1, 1), (0, 0), (0, 1)) if last else ((1, 0), (0, 0), (1, 1), (0, 1))
+            for n_bank, (c, h) in enumerate(order):
+                xc, xsc = x_codes[2 * bt + h]
+                ob = ps_o.tile([P, 512], F32, name="ob")
+                for ml in range(4):
+                    pairs = ((0, "r"), (1, "n")) if c == 0 else ((0, "i"), (1, "r"))
+                    for n, (s, v) in enumerate(pairs):
+                        sl = slice((4 * s + ml) * P, (4 * s + ml + 1) * P)
+                        wl = slice((4 * h + ml) * P, (4 * h + ml + 1) * P)
+                        nc.tensor.matmul_mx(
+                            out=ob[:, ml * P : (ml + 1) * P],
+                            lhsT=xc[:, sl].bitcast(FP8X4),
+                            lhsT_scale=xsc[:, sl],
+                            rhs=w_codes[(v, oh)][:, wl].bitcast(FP8X4),
+                            rhs_scale=w_scales[(v, oh)][:, wl],
+                            start=(n == 0),
+                            stop=(n == 1),
+                        )
+                o_ap = ot[:, c, :, 4 * h : 4 * h + 4]
+                i_ap = ob[:].rearrange("p (m o) -> p o m", m=4)
+                if c == 0 and oh == 0 and bt >= 2:
+                    nc.vector.tensor_copy(out=o_ap, in_=i_ap)
+                else:
+                    nc.scalar.copy(out=o_ap, in_=i_ap)
+                if last and n_bank == 1:
+                    store(ot, bt, oh, 1, 2)
+            if last:
+                store(ot, bt, oh, 0, 1)
+            else:
+                store(ot, bt, oh, 0, 2)
 
         load_x(0)
         load_w("i", 0)
@@ -170,13 +175,34 @@ def tile_mymodel_t_kernel(tc, x_real, x_imag, w_real, w_imag, out):
 
         tau(0)
         tau(1)
-        prep_w(0)
+        regroup_w("g", "i", 0, 0)
+        regroup_w("v", "r", 0, 0)
+        regroup_w("s", "i", 0, 1)
+        regroup_w("g", "r", 0, 1)
+        quant_w_half(0, 0)
+        quant_w_half(0, 1)
+        for h in range(2):
+            regroup_w("g", "i", 1, h)
+            regroup_w("g", "r", 1, h)
         tau(2)
-        for j in range(2 * NBT):
-            if 1 <= j and j + 2 < 2 * NBT:
-                tau(j + 2)
-            if j == 1:
-                prep_w(1)
-            mu(j)
-            if j % 2 == 1 and j // 2 + XBUFS < NBT:
-                load_x(j // 2 + XBUFS)
+        mu(0, 0, False)
+        tau(3)
+        tau(4)
+        mu(1, 0, False)
+        load_x(4)
+        quant_w_half(1, 0)
+        quant_w_half(1, 1)
+        tau(5)
+        mu(0, 1, False)
+        tau(6)
+        mu(1, 1, False)
+        load_x(5)
+        u = 7
+        for bt in range(2, NBT):
+            for oh in range(2):
+                if u < 2 * NBT:
+                    tau(u)
+                    u += 1
+                mu(bt, oh, bt == NBT - 1 and oh == 1)
+            if bt + 4 < NBT:
+                load_x(bt + 4)

@@ -24,8 +24,8 @@ def tile_mymodel_t_kernel(tc, x_real, x_imag, w_real, w_imag, out):
         x_imag.rearrange("b i x y z -> b (i x y z)"),
     ]
     w_dram = {
-        "r": w_real.rearrange("(t p) o x y z -> p t (o x y z)", p=P),
-        "i": w_imag.rearrange("(t p) o x y z -> p t (o x y z)", p=P),
+        "r": w_real.rearrange("(u p e) o x y z -> u p e (o x y z)", u=2, e=2),
+        "i": w_imag.rearrange("(u p e) o x y z -> u p e (o x y z)", u=2, e=2),
     }
     out_dram = out.rearrange("c b o x y z -> b c (o x y z)")
 
@@ -33,9 +33,10 @@ def tile_mymodel_t_kernel(tc, x_real, x_imag, w_real, w_imag, out):
         const = ctx.enter_context(tc.tile_pool(name="const", bufs=1))
         big = ctx.enter_context(tc.tile_pool(name="big", bufs=10))
         wpool = ctx.enter_context(tc.tile_pool(name="wpool", bufs=1))
+        spool = ctx.enter_context(tc.tile_pool(name="spool", bufs=4))
         gpool = ctx.enter_context(tc.tile_pool(name="gpool", bufs=2))
         cpool = ctx.enter_context(tc.tile_pool(name="cpool", bufs=8))
-        opool = ctx.enter_context(tc.tile_pool(name="opool", bufs=4))
+        opool = ctx.enter_context(tc.tile_pool(name="opool", bufs=3))
         ps_t = ctx.enter_context(tc.psum_pool(name="ps_t", bufs=4))
         ps_o = ctx.enter_context(tc.psum_pool(name="ps_o", bufs=4))
         ctx.enter_context(tc.manual_schedule())
@@ -55,7 +56,11 @@ def tile_mymodel_t_kernel(tc, x_real, x_imag, w_real, w_imag, out):
 
         def load_w(v, oh):
             wt = big.tile([P, 4, P * NM], BF16, name="wt", tag="big")
-            nc.sync.dma_start(out=wt[:], in_=w_dram[v][:, :, oh * P * NM : (oh + 1) * P * NM])
+            for u in range(2):
+                nc.sync.dma_start(
+                    out=wt[:, 2 * u : 2 * u + 2, :],
+                    in_=w_dram[v][u, :, :, oh * P * NM : (oh + 1) * P * NM],
+                )
             w_raw[(v, oh)] = wt
 
         w_codes = {}
@@ -95,6 +100,21 @@ def tile_mymodel_t_kernel(tc, x_real, x_imag, w_real, w_imag, out):
             quant_w("r", oh, h)
             quant_w("n", oh, h)
 
+        x_sorted = {}
+
+        def sort_x(u, s):
+            bt, h = u // 2, u % 2
+            xs = spool.tile([P, 4 * I], BF16, name="xs")
+            nc.gpsimd.tensor_scalar(
+                out=xs[:].rearrange("p (m i) -> p i m", m=4),
+                in0=x_tiles[(bt, s)][:].rearrange("p (i m) -> p i m", m=NM)[:, :, 4 * h : 4 * h + 4],
+                scalar1=1.0,
+                scalar2=0.0,
+                op0=MULT,
+                op1=ADD,
+            )
+            x_sorted[(u, s)] = xs
+
         x_codes = {}
 
         def tau(u):
@@ -102,19 +122,28 @@ def tile_mymodel_t_kernel(tc, x_real, x_imag, w_real, w_imag, out):
             grouped = gpool.tile([P, 4096], BF16, name="grouped", align_bytes=64)
             banks = []
             for s in range(2):
-                xw = x_tiles[(bt, s)][:].bitcast(F32).rearrange("p (i q) -> p i q", q=4)
+                if (u, s) in x_sorted:
+                    xw = x_sorted[(u, s)][:].bitcast(F32)
+                else:
+                    xw = x_tiles[(bt, s)][:].bitcast(F32).rearrange("p (u j e q) -> p u e q j", u=2, e=2, q=4)
                 for mpl in range(2):
                     tb = ps_t.tile([P, 512], F32, name="tb")
                     for t in range(4):
-                        nc.tensor.transpose(
-                            tb[:, t * P : (t + 1) * P],
-                            xw[:, t * P : (t + 1) * P, 2 * h + mpl],
-                            ident[:],
-                        )
+                        if (u, s) in x_sorted:
+                            col = (2 * mpl + t // 2) * 256 + (t % 2) * P
+                            src = xw[:, col : col + P]
+                        else:
+                            src = xw[:, t // 2, t % 2, 2 * h + mpl, :]
+                        nc.tensor.transpose(tb[:, t * P : (t + 1) * P], src, ident[:])
                     banks.append(tb)
             for k in range(4):
-                o_ap = grouped[:, k * 1024 : (k + 1) * 1024].rearrange("p (e b t) -> p e b t", e=2, t=4)
-                i_ap = banks[k][:].bitcast(BF16).rearrange("p (t b e) -> p e b t", t=4, e=2)
+                part = grouped[:, k * 1024 : (k + 1) * 1024]
+                if (u, k // 2) in x_sorted:
+                    o_ap = part.bitcast(F32).rearrange("p (m b u) -> p m b u", m=2, u=2)
+                    i_ap = banks[k][:].rearrange("p (m u b) -> p m b u", m=2, u=2)
+                else:
+                    o_ap = part.rearrange("p (m b t) -> p m b t", m=2, t=4)
+                    i_ap = banks[k][:].bitcast(BF16).rearrange("p (t b m) -> p m b t", t=4, m=2)
                 on_vector = (k == 3) if u < 6 else (k % 2 == 1)
                 if on_vector:
                     nc.vector.tensor_copy(out=o_ap, in_=i_ap)
@@ -192,8 +221,10 @@ def tile_mymodel_t_kernel(tc, x_real, x_imag, w_real, w_imag, out):
         load_x(4)
         quant_w_half(1, 0)
         quant_w_half(1, 1)
+        sort_x(6, 1)
         tau(5)
         mu(0, 1, False)
+        sort_x(7, 1)
         tau(6)
         mu(1, 1, False)
         load_x(5)
@@ -201,6 +232,8 @@ def tile_mymodel_t_kernel(tc, x_real, x_imag, w_real, w_imag, out):
         for bt in range(2, NBT):
             for oh in range(2):
                 if u < 2 * NBT:
+                    if u + 1 < 2 * NBT:
+                        sort_x(u + 1, 1)
                     tau(u)
                     u += 1
                 mu(bt, oh, bt == NBT - 1 and oh == 1)

@@ -82,7 +82,15 @@ def tile_mymodel_t_kernel(tc, x_real, x_imag, w_real, w_imag, out):
             elif eng == "s":
                 nc.scalar.copy(out=o_ap, in_=i_ap)
             else:
-                nc.gpsimd.tensor_scalar(out=o_ap, in0=i_ap, scalar1=1.0, scalar2=0.0, op0=MULT, op1=ADD)
+                for o0 in (0, P // 2):
+                    nc.gpsimd.tensor_scalar(
+                        out=o_ap[:, o0 : o0 + P // 2],
+                        in0=i_ap[:, o0 : o0 + P // 2],
+                        scalar1=1.0,
+                        scalar2=0.0,
+                        op0=MULT,
+                        op1=ADD,
+                    )
 
         def quant_w(v, oh, h):
             cols = slice(h * 512, (h + 1) * 512)
@@ -105,14 +113,17 @@ def tile_mymodel_t_kernel(tc, x_real, x_imag, w_real, w_imag, out):
         def sort_x(u, s):
             bt, h = u // 2, u % 2
             xs = spool.tile([P, 4 * I], BF16, name="xs")
-            nc.gpsimd.tensor_scalar(
-                out=xs[:].rearrange("p (m i) -> p i m", m=4),
-                in0=x_tiles[(bt, s)][:].rearrange("p (i m) -> p i m", m=NM)[:, :, 4 * h : 4 * h + 4],
-                scalar1=1.0,
-                scalar2=0.0,
-                op0=MULT,
-                op1=ADD,
-            )
+            o_ap = xs[:].rearrange("p (m i) -> p i m", m=4)
+            i_ap = x_tiles[(bt, s)][:].rearrange("p (i m) -> p i m", m=NM)[:, :, 4 * h : 4 * h + 4]
+            for i0 in (0, I // 2):
+                nc.gpsimd.tensor_scalar(
+                    out=o_ap[:, i0 : i0 + I // 2],
+                    in0=i_ap[:, i0 : i0 + I // 2],
+                    scalar1=1.0,
+                    scalar2=0.0,
+                    op0=MULT,
+                    op1=ADD,
+                )
             x_sorted[(u, s)] = xs
 
         x_codes = {}
@@ -215,10 +226,11 @@ def tile_mymodel_t_kernel(tc, x_real, x_imag, w_real, w_imag, out):
             regroup_w("g", "r", 1, h)
         tau(2)
         mu(0, 0, False)
+        load_x(4)
         tau(3)
         tau(4)
         mu(1, 0, False)
-        load_x(4)
+        load_x(5)
         quant_w_half(1, 0)
         quant_w_half(1, 1)
         sort_x(6, 1)
@@ -227,7 +239,7 @@ def tile_mymodel_t_kernel(tc, x_real, x_imag, w_real, w_imag, out):
         sort_x(7, 1)
         tau(6)
         mu(1, 1, False)
-        load_x(5)
+        load_x(6)
         u = 7
         for bt in range(2, NBT):
             for oh in range(2):
@@ -237,5 +249,5 @@ def tile_mymodel_t_kernel(tc, x_real, x_imag, w_real, w_imag, out):
                     tau(u)
                     u += 1
                 mu(bt, oh, bt == NBT - 1 and oh == 1)
-            if bt + 4 < NBT:
-                load_x(bt + 4)
+            if bt == 2:
+                load_x(7)

@@ -33,10 +33,10 @@ def tile_mymodel_t_kernel(tc, x_real, x_imag, w_real, w_imag, out):
         const = ctx.enter_context(tc.tile_pool(name="const", bufs=1))
         big = ctx.enter_context(tc.tile_pool(name="big", bufs=10))
         wpool = ctx.enter_context(tc.tile_pool(name="wpool", bufs=1))
-        spool = ctx.enter_context(tc.tile_pool(name="spool", bufs=4))
+        piece = ctx.enter_context(tc.tile_pool(name="piece", bufs=6))
         gpool = ctx.enter_context(tc.tile_pool(name="gpool", bufs=2))
         cpool = ctx.enter_context(tc.tile_pool(name="cpool", bufs=8))
-        opool = ctx.enter_context(tc.tile_pool(name="opool", bufs=3))
+        opool = ctx.enter_context(tc.tile_pool(name="opool", bufs=5))
         ps_t = ctx.enter_context(tc.psum_pool(name="ps_t", bufs=4))
         ps_o = ctx.enter_context(tc.psum_pool(name="ps_o", bufs=4))
         ctx.enter_context(tc.manual_schedule())
@@ -73,7 +73,7 @@ def tile_mymodel_t_kernel(tc, x_real, x_imag, w_real, w_imag, out):
         w_grouped = {}
 
         def regroup_w(eng, v, oh, h):
-            g = wpool.tile([P, 2048], BF16, name="g_%s%d" % (v, h), align_bytes=64)
+            g = piece.tile([P, 2048], BF16, name="g", tag="piece", align_bytes=64)
             w_grouped[(v, oh, h)] = g
             o_ap = g[:].rearrange("p (m o t) -> p o t m", m=4, t=4)
             i_ap = w_raw[(v, oh)][:].rearrange("p t (o m) -> p o t m", m=NM)[:, :, :, 4 * h : 4 * h + 4]
@@ -82,15 +82,7 @@ def tile_mymodel_t_kernel(tc, x_real, x_imag, w_real, w_imag, out):
             elif eng == "s":
                 nc.scalar.copy(out=o_ap, in_=i_ap)
             else:
-                for o0 in (0, P // 2):
-                    nc.gpsimd.tensor_scalar(
-                        out=o_ap[:, o0 : o0 + P // 2],
-                        in0=i_ap[:, o0 : o0 + P // 2],
-                        scalar1=1.0,
-                        scalar2=0.0,
-                        op0=MULT,
-                        op1=ADD,
-                    )
+                nc.gpsimd.tensor_scalar(out=o_ap, in0=i_ap, scalar1=1.0, scalar2=0.0, op0=MULT, op1=ADD)
 
         def quant_w(v, oh, h):
             cols = slice(h * 512, (h + 1) * 512)
@@ -102,7 +94,7 @@ def tile_mymodel_t_kernel(tc, x_real, x_imag, w_real, w_imag, out):
 
         def quant_w_half(oh, h):
             quant_w("i", oh, h)
-            gn = wpool.tile([P, 2048], BF16, name="g_n%d" % h, align_bytes=64)
+            gn = piece.tile([P, 2048], BF16, name="gn", tag="piece", align_bytes=64)
             w_grouped[("n", oh, h)] = gn
             nc.vector.tensor_scalar_mul(out=gn[:], in0=w_grouped[("i", oh, h)][:], scalar1=-1.0)
             quant_w("r", oh, h)
@@ -112,18 +104,15 @@ def tile_mymodel_t_kernel(tc, x_real, x_imag, w_real, w_imag, out):
 
         def sort_x(u, s):
             bt, h = u // 2, u % 2
-            xs = spool.tile([P, 4 * I], BF16, name="xs")
-            o_ap = xs[:].rearrange("p (m i) -> p i m", m=4)
-            i_ap = x_tiles[(bt, s)][:].rearrange("p (i m) -> p i m", m=NM)[:, :, 4 * h : 4 * h + 4]
-            for i0 in (0, I // 2):
-                nc.gpsimd.tensor_scalar(
-                    out=o_ap[:, i0 : i0 + I // 2],
-                    in0=i_ap[:, i0 : i0 + I // 2],
-                    scalar1=1.0,
-                    scalar2=0.0,
-                    op0=MULT,
-                    op1=ADD,
-                )
+            xs = piece.tile([P, 4 * I], BF16, name="xs", tag="piece", align_bytes=64)
+            nc.gpsimd.tensor_scalar(
+                out=xs[:].rearrange("p (m i) -> p i m", m=4),
+                in0=x_tiles[(bt, s)][:].rearrange("p (i m) -> p i m", m=NM)[:, :, 4 * h : 4 * h + 4],
+                scalar1=1.0,
+                scalar2=0.0,
+                op0=MULT,
+                op1=ADD,
+            )
             x_sorted[(u, s)] = xs
 
         x_codes = {}
@@ -193,7 +182,7 @@ def tile_mymodel_t_kernel(tc, x_real, x_imag, w_real, w_imag, out):
                         )
                 o_ap = ot[:, c, :, 4 * h : 4 * h + 4]
                 i_ap = ob[:].rearrange("p (m o) -> p o m", m=4)
-                if c == 0 and oh == 0 and bt >= 2:
+                if c == 0 and bt >= 2 and (oh == 0 or bt >= 6):
                     nc.vector.tensor_copy(out=o_ap, in_=i_ap)
                 else:
                     nc.scalar.copy(out=o_ap, in_=i_ap)
@@ -221,12 +210,13 @@ def tile_mymodel_t_kernel(tc, x_real, x_imag, w_real, w_imag, out):
         regroup_w("g", "r", 0, 1)
         quant_w_half(0, 0)
         quant_w_half(0, 1)
-        for h in range(2):
-            regroup_w("g", "i", 1, h)
-            regroup_w("g", "r", 1, h)
+        regroup_w("g", "i", 1, 0)
+        regroup_w("g", "r", 1, 0)
         tau(2)
         mu(0, 0, False)
         load_x(4)
+        regroup_w("v", "i", 1, 1)
+        regroup_w("v", "r", 1, 1)
         tau(3)
         tau(4)
         mu(1, 0, False)

@@ -33,10 +33,10 @@ def tile_mymodel_t_kernel(tc, x_real, x_imag, w_real, w_imag, out):
         const = ctx.enter_context(tc.tile_pool(name="const", bufs=1))
         big = ctx.enter_context(tc.tile_pool(name="big", bufs=10))
         wpool = ctx.enter_context(tc.tile_pool(name="wpool", bufs=1))
-        piece = ctx.enter_context(tc.tile_pool(name="piece", bufs=6))
+        spool = ctx.enter_context(tc.tile_pool(name="spool", bufs=4))
         gpool = ctx.enter_context(tc.tile_pool(name="gpool", bufs=2))
         cpool = ctx.enter_context(tc.tile_pool(name="cpool", bufs=8))
-        opool = ctx.enter_context(tc.tile_pool(name="opool", bufs=5))
+        opool = ctx.enter_context(tc.tile_pool(name="opool", bufs=3))
         ps_t = ctx.enter_context(tc.psum_pool(name="ps_t", bufs=4))
         ps_o = ctx.enter_context(tc.psum_pool(name="ps_o", bufs=4))
         ctx.enter_context(tc.manual_schedule())
@@ -73,7 +73,7 @@ def tile_mymodel_t_kernel(tc, x_real, x_imag, w_real, w_imag, out):
         w_grouped = {}
 
         def regroup_w(eng, v, oh, h):
-            g = piece.tile([P, 2048], BF16, name="g", tag="piece", align_bytes=64)
+            g = wpool.tile([P, 2048], BF16, name="g_%s%d" % (v, h), align_bytes=64)
             w_grouped[(v, oh, h)] = g
             o_ap = g[:].rearrange("p (m o t) -> p o t m", m=4, t=4)
             i_ap = w_raw[(v, oh)][:].rearrange("p t (o m) -> p o t m", m=NM)[:, :, :, 4 * h : 4 * h + 4]
@@ -94,7 +94,7 @@ def tile_mymodel_t_kernel(tc, x_real, x_imag, w_real, w_imag, out):
 
         def quant_w_half(oh, h):
             quant_w("i", oh, h)
-            gn = piece.tile([P, 2048], BF16, name="gn", tag="piece", align_bytes=64)
+            gn = wpool.tile([P, 2048], BF16, name="g_n%d" % h, align_bytes=64)
             w_grouped[("n", oh, h)] = gn
             nc.vector.tensor_scalar_mul(out=gn[:], in0=w_grouped[("i", oh, h)][:], scalar1=-1.0)
             quant_w("r", oh, h)
@@ -104,7 +104,7 @@ def tile_mymodel_t_kernel(tc, x_real, x_imag, w_real, w_imag, out):
 
         def sort_x(u, s):
             bt, h = u // 2, u % 2
-            xs = piece.tile([P, 4 * I], BF16, name="xs", tag="piece", align_bytes=64)
+            xs = spool.tile([P, 4 * I], BF16, name="xs")
             nc.gpsimd.tensor_scalar(
                 out=xs[:].rearrange("p (m i) -> p i m", m=4),
                 in0=x_tiles[(bt, s)][:].rearrange("p (i m) -> p i m", m=NM)[:, :, 4 * h : 4 * h + 4],
@@ -117,11 +117,15 @@ def tile_mymodel_t_kernel(tc, x_real, x_imag, w_real, w_imag, out):
 
         x_codes = {}
 
-        def tau(u):
+        x_grouped = {}
+
+        def tau_half(u, s_half):
             bt, h = u // 2, u % 2
-            grouped = gpool.tile([P, 4096], BF16, name="grouped", align_bytes=64)
-            banks = []
-            for s in range(2):
+            if s_half == 0:
+                x_grouped[u] = gpool.tile([P, 4096], BF16, name="grouped", align_bytes=64)
+            grouped = x_grouped[u]
+            banks = {}
+            for s in (s_half,):
                 if (u, s) in x_sorted:
                     xw = x_sorted[(u, s)][:].bitcast(F32)
                 else:
@@ -135,8 +139,8 @@ def tile_mymodel_t_kernel(tc, x_real, x_imag, w_real, w_imag, out):
                         else:
                             src = xw[:, t // 2, t % 2, 2 * h + mpl, :]
                         nc.tensor.transpose(tb[:, t * P : (t + 1) * P], src, ident[:])
-                    banks.append(tb)
-            for k in range(4):
+                    banks[2 * s + mpl] = tb
+            for k in (2 * s_half, 2 * s_half + 1):
                 part = grouped[:, k * 1024 : (k + 1) * 1024]
                 if (u, k // 2) in x_sorted:
                     o_ap = part.bitcast(F32).rearrange("p (m b u) -> p m b u", m=2, u=2)
@@ -149,10 +153,15 @@ def tile_mymodel_t_kernel(tc, x_real, x_imag, w_real, w_imag, out):
                     nc.vector.tensor_copy(out=o_ap, in_=i_ap)
                 else:
                     nc.scalar.copy(out=o_ap, in_=i_ap)
-            xc = cpool.tile([P, 1024], U32, name="xc", align_bytes=64)
-            xsc = cpool.tile([P, 1024], U8, name="xsc", align_bytes=64)
-            nc.vector.quantize_mx(out=xc[:].bitcast(FP8X4), scales=xsc[:], in_=grouped[:])
-            x_codes[u] = (xc, xsc)
+            if s_half == 1:
+                xc = cpool.tile([P, 1024], U32, name="xc", align_bytes=64)
+                xsc = cpool.tile([P, 1024], U8, name="xsc", align_bytes=64)
+                nc.vector.quantize_mx(out=xc[:].bitcast(FP8X4), scales=xsc[:], in_=grouped[:])
+                x_codes[u] = (xc, xsc)
+
+        def tau(u):
+            tau_half(u, 0)
+            tau_half(u, 1)
 
         def store(ot, bt, oh, c0, c1):
             nc.sync.dma_start(
@@ -160,10 +169,12 @@ def tile_mymodel_t_kernel(tc, x_real, x_imag, w_real, w_imag, out):
                 in_=ot[:, c0:c1].rearrange("p c o m -> p c (o m)"),
             )
 
-        def mu(bt, oh, last):
+        def mu(bt, oh, last, woven=None):
             ot = opool.tile([P, 2, P, NM], F32, name="ot")
             order = ((1, 0), (1, 1), (0, 0), (0, 1)) if last else ((1, 0), (0, 0), (1, 1), (0, 1))
             for n_bank, (c, h) in enumerate(order):
+                if woven is not None and n_bank % 2 == 0:
+                    tau_half(woven, n_bank // 2)
                 xc, xsc = x_codes[2 * bt + h]
                 ob = ps_o.tile([P, 512], F32, name="ob")
                 for ml in range(4):
@@ -182,7 +193,7 @@ def tile_mymodel_t_kernel(tc, x_real, x_imag, w_real, w_imag, out):
                         )
                 o_ap = ot[:, c, :, 4 * h : 4 * h + 4]
                 i_ap = ob[:].rearrange("p (m o) -> p o m", m=4)
-                if c == 0 and bt >= 2 and (oh == 0 or bt >= 6):
+                if c == 0 and oh == 0 and bt >= 2:
                     nc.vector.tensor_copy(out=o_ap, in_=i_ap)
                 else:
                     nc.scalar.copy(out=o_ap, in_=i_ap)
@@ -210,34 +221,30 @@ def tile_mymodel_t_kernel(tc, x_real, x_imag, w_real, w_imag, out):
         regroup_w("g", "r", 0, 1)
         quant_w_half(0, 0)
         quant_w_half(0, 1)
-        regroup_w("g", "i", 1, 0)
-        regroup_w("g", "r", 1, 0)
+        for h in range(2):
+            regroup_w("g", "i", 1, h)
+            regroup_w("g", "r", 1, h)
         tau(2)
         mu(0, 0, False)
-        load_x(4)
-        regroup_w("v", "i", 1, 1)
-        regroup_w("v", "r", 1, 1)
         tau(3)
-        tau(4)
-        mu(1, 0, False)
-        load_x(5)
+        mu(1, 0, False, 4)
+        load_x(4)
         quant_w_half(1, 0)
         quant_w_half(1, 1)
         sort_x(6, 1)
-        tau(5)
-        mu(0, 1, False)
+        mu(0, 1, False, 5)
         sort_x(7, 1)
-        tau(6)
-        mu(1, 1, False)
-        load_x(6)
+        mu(1, 1, False, 6)
+        load_x(5)
         u = 7
         for bt in range(2, NBT):
             for oh in range(2):
+                woven = None
                 if u < 2 * NBT:
                     if u + 1 < 2 * NBT:
                         sort_x(u + 1, 1)
-                    tau(u)
+                    woven = u
                     u += 1
-                mu(bt, oh, bt == NBT - 1 and oh == 1)
-            if bt == 2:
-                load_x(7)
+                mu(bt, oh, bt == NBT - 1 and oh == 1, woven)
+            if bt + 4 < NBT:
+                load_x(bt + 4)

from contextlib import ExitStack

import concourse.mybir as mybir
from concourse.masks import make_identity

F32 = mybir.dt.float32
BF16 = mybir.dt.bfloat16
U32 = mybir.dt.uint32
U8 = mybir.dt.uint8
FP8X4 = mybir.dt.float8_e4m3fn_x4
MULT = mybir.AluOpType.mult
ADD = mybir.AluOpType.add

P = 128
B, I, O, NM = 1024, 512, 256, 8
NBT = B // P
FLOPS = 2 * 4 * NM * B * I * O


def tile_mymodel_t_kernel(tc, x_real, x_imag, w_real, w_imag, out):
    nc = tc.nc
    xs_dram = [
        x_real.rearrange("b i x y z -> b (i x y z)"),
        x_imag.rearrange("b i x y z -> b (i x y z)"),
    ]
    w_dram = {
        "r": w_real.rearrange("(u p e) o x y z -> u p e (o x y z)", u=2, e=2),
        "i": w_imag.rearrange("(u p e) o x y z -> u p e (o x y z)", u=2, e=2),
    }
    out_dram = out.rearrange("c b o x y z -> b c (o x y z)")

    with ExitStack() as ctx:
        const = ctx.enter_context(tc.tile_pool(name="const", bufs=1))
        big = ctx.enter_context(tc.tile_pool(name="big", bufs=10))
        wpool = ctx.enter_context(tc.tile_pool(name="wpool", bufs=1))
        spool = ctx.enter_context(tc.tile_pool(name="spool", bufs=4))
        gpool = ctx.enter_context(tc.tile_pool(name="gpool", bufs=2))
        cpool = ctx.enter_context(tc.tile_pool(name="cpool", bufs=8))
        opool = ctx.enter_context(tc.tile_pool(name="opool", bufs=3))
        ps_t = ctx.enter_context(tc.psum_pool(name="ps_t", bufs=4))
        ps_o = ctx.enter_context(tc.psum_pool(name="ps_o", bufs=4))
        ctx.enter_context(tc.manual_schedule())

        ident = const.tile([P, P], F32, name="ident")
        make_identity(nc, ident[:])

        x_tiles = {}

        def load_x(bt):
            for s in range(2):
                xt = big.tile([P, I * NM], BF16, name="xt", tag="big")
                nc.sync.dma_start(out=xt[:], in_=xs_dram[s][bt * P : (bt + 1) * P, :])
                x_tiles[(bt, s)] = xt

        w_raw = {}

        def load_w(v, oh):
            wt = big.tile([P, 4, P * NM], BF16, name="wt", tag="big")
            for u in range(2):
                nc.sync.dma_start(
                    out=wt[:, 2 * u : 2 * u + 2, :],
                    in_=w_dram[v][u, :, :, oh * P * NM : (oh + 1) * P * NM],
                )
            w_raw[(v, oh)] = wt

        w_codes = {}
        w_scales = {}
        for v in ("r", "i", "n"):
            for oh in range(2):
                w_codes[(v, oh)] = wpool.tile([P, NM * P], U32, name="wc_%s%d" % (v, oh), align_bytes=64)
                w_scales[(v, oh)] = wpool.tile([P, NM * P], U8, name="ws_%s%d" % (v, oh), align_bytes=64)

        w_grouped = {}

        def regroup_w(eng, v, oh, h):
            g = wpool.tile([P, 2048], BF16, name="g_%s%d" % (v, h), align_bytes=64)
            w_grouped[(v, oh, h)] = g
            o_ap = g[:].rearrange("p (m o t) -> p o t m", m=4, t=4)
            i_ap = w_raw[(v, oh)][:].rearrange("p t (o m) -> p o t m", m=NM)[:, :, :, 4 * h : 4 * h + 4]
            if eng == "v":
                nc.vector.tensor_copy(out=o_ap, in_=i_ap)
            elif eng == "s":
                nc.scalar.copy(out=o_ap, in_=i_ap)
            else:
                nc.gpsimd.tensor_scalar(out=o_ap, in0=i_ap, scalar1=1.0, scalar2=0.0, op0=MULT, op1=ADD)

        def quant_w(v, oh, h):
            cols = slice(h * 512, (h + 1) * 512)
            nc.vector.quantize_mx(
                out=w_codes[(v, oh)][:, cols].bitcast(FP8X4),
                scales=w_scales[(v, oh)][:, cols],
                in_=w_grouped[(v, oh, h)][:],
            )

        def quant_w_half(oh, h):
            quant_w("i", oh, h)
            gn = wpool.tile([P, 2048], BF16, name="g_n%d" % h, align_bytes=64)
            w_grouped[("n", oh, h)] = gn
            nc.vector.tensor_scalar_mul(out=gn[:], in0=w_grouped[("i", oh, h)][:], scalar1=-1.0)
            quant_w("r", oh, h)
            quant_w("n", oh, h)

        x_sorted = {}

        def sort_x(u, s):
            bt, h = u // 2, u % 2
            xs = spool.tile([P, 4 * I], BF16, name="xs")
            nc.gpsimd.tensor_scalar(
                out=xs[:].rearrange("p (m i) -> p i m", m=4),
                in0=x_tiles[(bt, s)][:].rearrange("p (i m) -> p i m", m=NM)[:, :, 4 * h : 4 * h + 4],
                scalar1=1.0,
                scalar2=0.0,
                op0=MULT,
                op1=ADD,
            )
            x_sorted[(u, s)] = xs

        x_codes = {}

        x_grouped = {}

        def tau_half(u, s_half):
            bt, h = u // 2, u % 2
            if s_half == 0:
                x_grouped[u] = gpool.tile([P, 4096], BF16, name="grouped", align_bytes=64)
            grouped = x_grouped[u]
            banks = {}
            for s in (s_half,):
                if (u, s) in x_sorted:
                    xw = x_sorted[(u, s)][:].bitcast(F32)
                else:
                    xw = x_tiles[(bt, s)][:].bitcast(F32).rearrange("p (u j e q) -> p u e q j", u=2, e=2, q=4)
                for mpl in range(2):
                    tb = ps_t.tile([P, 512], F32, name="tb")
                    for t in range(4):
                        if (u, s) in x_sorted:
                            col = (2 * mpl + t // 2) * 256 + (t % 2) * P
                            src = xw[:, col : col + P]
                        else:
                            src = xw[:, t // 2, t % 2, 2 * h + mpl, :]
                        nc.tensor.transpose(tb[:, t * P : (t + 1) * P], src, ident[:])
                    banks[2 * s + mpl] = tb
            for k in (2 * s_half, 2 * s_half + 1):
                part = grouped[:, k * 1024 : (k + 1) * 1024]
                if (u, k // 2) in x_sorted:
                    o_ap = part.bitcast(F32).rearrange("p (m b u) -> p m b u", m=2, u=2)
                    i_ap = banks[k][:].rearrange("p (m u b) -> p m b u", m=2, u=2)
                else:
                    o_ap = part.rearrange("p (m b t) -> p m b t", m=2, t=4)
                    i_ap = banks[k][:].bitcast(BF16).rearrange("p (t b m) -> p m b t", t=4, m=2)
                on_vector = (k == 3) if u < 6 else (k % 2 == 1)
                if on_vector:
                    nc.vector.tensor_copy(out=o_ap, in_=i_ap)
                else:
                    nc.scalar.copy(out=o_ap, in_=i_ap)
            if s_half == 1:
                xc = cpool.tile([P, 1024], U32, name="xc", align_bytes=64)
                xsc = cpool.tile([P, 1024], U8, name="xsc", align_bytes=64)
                nc.vector.quantize_mx(out=xc[:].bitcast(FP8X4), scales=xsc[:], in_=grouped[:])
                x_codes[u] = (xc, xsc)

        def tau(u):
            tau_half(u, 0)
            tau_half(u, 1)

        def store(ot, bt, oh, c0, c1):
            nc.sync.dma_start(
                out=out_dram[bt * P : (bt + 1) * P, c0:c1, oh * P * NM : (oh + 1) * P * NM],
                in_=ot[:, c0:c1].rearrange("p c o m -> p c (o m)"),
            )

        def mu(bt, oh, last, woven=None):
            ot = opool.tile([P, 2, P, NM], F32, name="ot")
            order = ((1, 0), (1, 1), (0, 0), (0, 1)) if last else ((1, 0), (0, 0), (1, 1), (0, 1))
            for n_bank, (c, h) in enumerate(order):
                if woven is not None and n_bank % 2 == 0:
                    tau_half(woven, n_bank // 2)
                xc, xsc = x_codes[2 * bt + h]
                ob = ps_o.tile([P, 512], F32, name="ob")
                for ml in range(4):
                    pairs = ((0, "r"), (1, "n")) if c == 0 else ((0, "i"), (1, "r"))
                    for n, (s, v) in enumerate(pairs):
                        sl = slice((4 * s + ml) * P, (4 * s + ml + 1) * P)
                        wl = slice((4 * h + ml) * P, (4 * h + ml + 1) * P)
                        nc.tensor.matmul_mx(
                            out=ob[:, ml * P : (ml + 1) * P],
                            lhsT=xc[:, sl].bitcast(FP8X4),
                            lhsT_scale=xsc[:, sl],
                            rhs=w_codes[(v, oh)][:, wl].bitcast(FP8X4),
                            rhs_scale=w_scales[(v, oh)][:, wl],
                            start=(n == 0),
                            stop=(n == 1),
                        )
                o_ap = ot[:, c, :, 4 * h : 4 * h + 4]
                i_ap = ob[:].rearrange("p (m o) -> p o m", m=4)
                if c == 0 and oh == 0 and bt >= 2:
                    nc.vector.tensor_copy(out=o_ap, in_=i_ap)
                else:
                    nc.scalar.copy(out=o_ap, in_=i_ap)
                if last and n_bank == 1:
                    store(ot, bt, oh, 1, 2)
            if last:
                store(ot, bt, oh, 0, 1)
            else:
                store(ot, bt, oh, 0, 2)

        load_x(0)
        load_w("i", 0)
        load_w("r", 0)
        load_x(1)
        load_w("i", 1)
        load_w("r", 1)
        load_x(2)
        load_x(3)

        tau(0)
        tau(1)
        regroup_w("g", "i", 0, 0)
        regroup_w("v", "r", 0, 0)
        regroup_w("s", "i", 0, 1)
        regroup_w("g", "r", 0, 1)
        quant_w_half(0, 0)
        quant_w_half(0, 1)
        for h in range(2):
            regroup_w("g", "i", 1, h)
            regroup_w("g", "r", 1, h)
        tau(2)
        mu(0, 0, False)
        tau(3)
        mu(1, 0, False, 4)
        load_x(4)
        quant_w_half(1, 0)
        quant_w_half(1, 1)
        sort_x(6, 1)
        mu(0, 1, False, 5)
        sort_x(7, 1)
        mu(1, 1, False, 6)
        load_x(5)
        u = 7
        for bt in range(2, NBT):
            for oh in range(2):
                woven = None
                if u < 2 * NBT:
                    if u + 1 < 2 * NBT:
                        sort_x(u + 1, 1)
                    woven = u
                    u += 1
                mu(bt, oh, bt == NBT - 1 and oh == 1, woven)
            if bt + 4 < NBT:
                load_x(bt + 4)
